import numpy as np
import ml_dtypes


def mxq(x, axis, fmt="e4m3"):
    dtype, down = {"e4m3": (ml_dtypes.float8_e4m3fn, 7), "e5m2": (ml_dtypes.float8_e5m2, 14)}[fmt]
    v = np.moveaxis(np.asarray(x, np.float32).astype(ml_dtypes.bfloat16).astype(np.float64), axis, -1)
    blocks = v.reshape(v.shape[:-1] + (-1, 32))
    amax = np.abs(blocks).max(-1, keepdims=True)
    byte = np.maximum(np.where(amax > 0, np.frexp(amax)[1] - 1 + 127, 0) - down, 1)
    scale = np.exp2(byte - 127.0)
    codes = (blocks / scale).astype(np.float32).astype(dtype).astype(np.float64)
    return np.moveaxis((codes * scale).reshape(v.shape), -1, axis)


WIDE = False


def mx_kscale(k):
    if not WIDE:
        return np.ones(k)
    levels = np.array([10, -10, 5, -5, 0])
    a = np.random.permutation(np.resize(levels, k // 512 * 4)).reshape(k // 512, 4)
    idx = np.arange(k)
    return np.exp2(a[idx // 512, idx % 128 // 32])


BF16 = ml_dtypes.bfloat16


def bf(x):
    return np.asarray(x, np.float32).astype(BF16)


def f64(x):
    return np.asarray(x).astype(np.float64)


E2M1 = np.array([0.0, 0.5, 1.0, 1.5, 2.0, 3.0, 4.0, 6.0, -0.0, -0.5, -1.0, -1.5, -2.0, -3.0, -4.0, -6.0])


def pack_weight(w, fmt):
    k, n = w.shape
    w = f64(bf(w)).reshape(k // 32, 32, n)
    amax = np.abs(w).max(1)
    if fmt == "e4m3":
        byte = np.frexp(amax)[1] - 1 + 127 - 7
    else:
        mant, ex = np.frexp(amax / 6.0)
        byte = np.where(mant > 0.5, ex, ex - 1) + 127
    byte = np.clip(np.where(amax > 0, byte, 1), 1, 254)
    scaled = (w * np.exp2(127.0 - byte)[:, None, :]).reshape(k, n).astype(np.float32)
    by_word = np.ascontiguousarray(scaled.reshape(k // 512, 128, 4, n).transpose(0, 1, 3, 2))
    if fmt == "e4m3":
        words = by_word.astype(ml_dtypes.float8_e4m3fn).view(np.uint8)
    else:
        c = by_word.astype(ml_dtypes.float4_e2m1fn).view(np.uint8) & 0xF
        words = c[..., 0::2] | (c[..., 1::2] << 4)
    return np.ascontiguousarray(words), np.ascontiguousarray(byte.astype(np.uint8).reshape(k // 512, 16, n))


def unpack_weight(words, scales, fmt):
    g, p, n, _ = words.shape
    if fmt == "e4m3":
        vals = np.ascontiguousarray(words).view(ml_dtypes.float8_e4m3fn).astype(np.float64)
    else:
        nib = np.empty((g, p, n, 4), np.uint8)
        nib[..., 0::2] = words & 0xF
        nib[..., 1::2] = words >> 4
        vals = E2M1[nib]
    vals = vals * np.repeat(np.exp2(scales.astype(np.float64) - 127.0), 8, axis=1)[..., None]
    return vals.transpose(0, 1, 3, 2).reshape(g * 512, n)


B, H, W, C, NH, D = 2, 32, 32, 512, 4, 128
K_SIZE = 5
PAD = K_SIZE // 2


def softmax(v):
    e = np.exp(v - v.max(-1, keepdims=True))
    return e / e.sum(-1, keepdims=True)


def setup_inputs():
    s = mx_kscale(C)
    main = bf(np.random.standard_normal((B, H, W, C)) * s)
    ref = bf(np.random.standard_normal((B, H, W, C)) * s)
    w_main = np.random.standard_normal((NH, C, D)) * 1.5 / np.sqrt(C * D) / s[:, None]
    w_ref = np.random.standard_normal((NH, C, D)) * 1.0 / np.sqrt(C) / s[:, None]
    W_main_words, W_main_scales = pack_weight(w_main.reshape(-1, D), "e4m3")
    W_ref_words, W_ref_scales = pack_weight(w_ref.reshape(-1, D), "e4m3")
    return {"main": main,
            "ref": ref,
            "W_main_words": W_main_words, "W_main_scales": W_main_scales,
            "W_ref_words": W_ref_words, "W_ref_scales": W_ref_scales}


def reference(main, ref, W_main_words, W_main_scales, W_ref_words, W_ref_scales):
    q = (mxq(f64(main), 3, "e4m3").reshape(B * H * W, C) @ unpack_weight(W_main_words, W_main_scales, "e4m3").reshape(NH, C, D)).reshape(NH, B, H, W, D)
    k = (mxq(f64(ref), 3, "e4m3").reshape(B * H * W, C) @ unpack_weight(W_ref_words, W_ref_scales, "e4m3").reshape(NH, C, D)).reshape(NH, B, H, W, D)
    kp = np.pad(k, ((0, 0), (0, 0), (PAD, PAD), (PAD, PAD), (0, 0)))
    scores = [np.sum(q * kp[:, :, di:di + H, dj:dj + W, :], axis=-1) for di in range(K_SIZE) for dj in range(K_SIZE)]
    scores.append(np.sum(q * q, axis=-1))
    attn = softmax(np.stack(scores, axis=-1))
    return np.mean(attn, axis=0)

@@ -1,0 +1,222 @@
+from contextlib import ExitStack
+
+import concourse.mybir as mybir
+from concourse.masks import make_identity
+
+F32 = mybir.dt.float32
+BF16 = mybir.dt.bfloat16
+I32 = mybir.dt.int32
+U32 = mybir.dt.uint32
+U8 = mybir.dt.uint8
+FP8X4 = mybir.dt.float8_e4m3fn_x4
+ALU = mybir.AluOpType
+ACT = mybir.ActivationFunctionType
+AX = mybir.AxisListType
+
+P = 128
+B, H, W, C, NH, D = 2, 32, 32, 512, 4, 128
+WIN = 5
+PAD = WIN // 2
+NT = WIN * WIN + 1
+PIXELS = B * H * W
+CHUNK = 512
+N_CHUNKS = PIXELS // CHUNK
+CHUNKS_IMAGE = N_CHUNKS // B
+BLOCKS = CHUNK // P
+ROWS_CHUNK = CHUNK // W
+HP = H + 2 * PAD
+WP = W + 2 * PAD
+PAIRS = NH // 2
+
+FLOPS = 2 * 2 * PIXELS * C * NH * D + 2 * NH * PIXELS * NT * D
+
+
+def tile_reflocal7mh_e_kernel(
+    tc, main, ref, W_main_words, W_main_scales, W_ref_words, W_ref_scales, out
+):
+    nc = tc.nc
+    x_rows = {
+        "ref": ref.rearrange("b i j c -> (b i j) c"),
+        "main": main.rearrange("b i j c -> (b i j) c"),
+    }
+    out_rows = out.rearrange("b i j t -> (b i j) t")
+
+    with ExitStack() as ctx:
+        const = ctx.enter_context(tc.tile_pool(name="const", bufs=1))
+        xpool = ctx.enter_context(tc.tile_pool(name="xpool", bufs=2 * N_CHUNKS))
+        stage = ctx.enter_context(tc.tile_pool(name="stage", bufs=2))
+        products = ctx.enter_context(tc.tile_pool(name="products", bufs=4))
+        soft = ctx.enter_context(tc.tile_pool(name="soft", bufs=2))
+        ps_xt = ctx.enter_context(tc.psum_pool(name="ps_xt", bufs=2))
+        ps_proj = ctx.enter_context(tc.psum_pool(name="ps_proj", bufs=2))
+        ps_score = ctx.enter_context(tc.psum_pool(name="ps_score", bufs=4))
+
+        def load_x(label, ch):
+            x_sb = xpool.tile([P, BLOCKS, C], BF16)
+            nc.sync.dma_start(
+                out=x_sb[:],
+                in_=x_rows[label][CHUNK * ch : CHUNK * (ch + 1), :].rearrange(
+                    "(k p) c -> p k c", p=P
+                ),
+            )
+            return x_sb
+
+        def load_weight(words, scales, label):
+            codes = const.tile([P, NH, D], U32, align_bytes=64, name="codes_" + label)
+            nc.sync.dma_start(
+                out=codes[:].bitcast(I32),
+                in_=words.rearrange("g p n t -> g p (n t)").bitcast(I32).rearrange("g p n -> p g n"),
+            )
+            plane = const.tile([P, NH, D], U8, align_bytes=64, name="plane_" + label)
+            nc.vector.memset(plane[:].bitcast(I32), 0)
+            scale_words = scales.bitcast(I32)
+            for quad in range(4):
+                nc.sync.dma_start(
+                    out=plane[:].bitcast(I32)[32 * quad : 32 * quad + 4, :, :],
+                    in_=scale_words[:, 4 * quad : 4 * quad + 4, :].rearrange("g r n -> r g n"),
+                )
+            return codes, plane
+
+        w_inputs = {"ref": (W_ref_words, W_ref_scales), "main": (W_main_words, W_main_scales)}
+        x_tiles = {}
+        weights = {}
+        for b in range(B):
+            for label in ("ref", "main"):
+                for ch in range(CHUNKS_IMAGE * b, CHUNKS_IMAGE * (b + 1)):
+                    x_tiles[(label, ch)] = load_x(label, ch)
+                    if ch == 0:
+                        weights[label] = load_weight(w_inputs[label][0], w_inputs[label][1], label)
+
+        ident = const.tile([P, P], F32)
+        make_identity(nc, ident[:])
+        ones = const.tile([P, 2], F32)
+        nc.gpsimd.memset(ones[:], 1.0)
+        x_codes = {}
+        x_planes = {}
+        for label in ("ref", "main"):
+            x_codes[label] = const.tile([P, PIXELS], U32, align_bytes=64, name="xcodes_" + label)
+            x_planes[label] = const.tile([P, PIXELS], U8, align_bytes=64, name="xplane_" + label)
+        q_sb = const.tile([P, NH, PIXELS], F32)
+        k_sb = const.tile([P, NH * B, HP * WP], F32)
+        nc.vector.memset(k_sb[:], 0.0)
+        result = const.tile([P, N_CHUNKS * BLOCKS, NT], F32)
+
+        def k_image(n, b):
+            return k_sb[:, n * B + b, :].rearrange("p (i j) -> p i j", j=WP)
+
+        def quantise(label, ch):
+            words = x_tiles[(label, ch)][:].bitcast(F32)
+            grouped = stage.tile([P, 4 * CHUNK], BF16, align_bytes=64)
+            grouped_words = grouped[:].bitcast(F32).rearrange("p (k r u) -> p k r u", r=P, u=2)
+            for half in range(BLOCKS // 2):
+                xt = ps_xt.tile([P, 2, 2, P], F32)
+                for k in range(2):
+                    for u in range(2):
+                        nc.tensor.transpose(
+                            xt[:, k, u, :], words[:, 2 * half + k, u : C // 2 : 2], ident[:]
+                        )
+                nc.scalar.copy(
+                    out=grouped_words[:, 2 * half : 2 * half + 2, :, :],
+                    in_=xt[:].rearrange("p k u r -> p k r u"),
+                )
+            cols = slice(CHUNK * ch, CHUNK * (ch + 1))
+            nc.vector.quantize_mx(
+                out=x_codes[label][:, cols].bitcast(FP8X4),
+                scales=x_planes[label][:, cols],
+                in_=grouped[:],
+            )
+
+        def project(label, ch):
+            quantise(label, ch)
+            cols = slice(CHUNK * ch, CHUNK * (ch + 1))
+            b, part = divmod(ch, CHUNKS_IMAGE)
+            rows = slice(PAD + ROWS_CHUNK * part, PAD + ROWS_CHUNK * (part + 1))
+            codes, plane = weights[label]
+            for n in range(NH):
+                acc = ps_proj.tile([P, CHUNK], F32)
+                nc.tensor.matmul_mx(
+                    out=acc[:],
+                    lhsT=codes[:, n, :].bitcast(FP8X4),
+                    lhsT_scale=plane[:, n, :],
+                    rhs=x_codes[label][:, cols].bitcast(FP8X4),
+                    rhs_scale=x_planes[label][:, cols],
+                    start=True,
+                    stop=True,
+                )
+                if label == "ref":
+                    nc.scalar.copy(
+                        out=k_image(n, b)[:, rows, PAD : PAD + W],
+                        in_=acc[:].rearrange("p (i j) -> p i j", j=W),
+                    )
+                else:
+                    nc.scalar.copy(out=q_sb[:, n, cols], in_=acc[:])
+
+        def attention(ch):
+            cols = slice(CHUNK * ch, CHUNK * (ch + 1))
+            b, part = divmod(ch, CHUNKS_IMAGE)
+            top = ROWS_CHUNK * part
+            scores = soft.tile([P, NH, NT, BLOCKS], F32)
+            for pair in range(PAIRS):
+                s_ps = ps_score.tile([P, 2, NT, BLOCKS, 2], F32)
+                for i in range(2):
+                    n = 2 * pair + i
+                    for t in range(NT):
+                        prod = products.tile([P, CHUNK], F32)
+                        if t < NT - 1:
+                            di, dj = divmod(t, WIN)
+                            nc.vector.tensor_tensor(
+                                out=prod[:].rearrange("p (i j) -> p i j", j=W),
+                                in0=q_sb[:, n, cols].rearrange("p (i j) -> p i j", j=W),
+                                in1=k_image(n, b)[:, top + di : top + di + ROWS_CHUNK, dj : dj + W],
+                                op=ALU.mult,
+                            )
+                        else:
+                            nc.scalar.activation(out=prod[:], in_=q_sb[:, n, cols], func=ACT.Square)
+                        for k in range(BLOCKS):
+                            nc.tensor.matmul(
+                                out=s_ps[:, i, t, k, :], lhsT=prod[:, P * k : P * (k + 1)], rhs=ones[:],
+                                start=True, stop=True,
+                            )
+                nc.scalar.copy(out=scores[:, 2 * pair : 2 * pair + 2, :, :], in_=s_ps[:, :, :, :, 0])
+            by_t = "p n t k -> p n k t"
+            spread = [P, NH, NT, BLOCKS]
+            neg_max = soft.tile([P, NH, BLOCKS], F32)
+            nc.vector.tensor_reduce(
+                out=neg_max[:], in_=scores[:].rearrange(by_t), axis=AX.X, op=ALU.max, negate=True
+            )
+            shifted = soft.tile(spread, F32)
+            nc.vector.tensor_tensor(
+                out=shifted[:], in0=scores[:], in1=neg_max[:].unsqueeze(2).to_broadcast(spread),
+                op=ALU.add,
+            )
+            expd = soft.tile(spread, F32)
+            nc.scalar.activation(out=expd[:], in_=shifted[:], func=ACT.Exp)
+            total = soft.tile([P, NH, BLOCKS], F32)
+            nc.vector.tensor_reduce(out=total[:], in_=expd[:].rearrange(by_t), axis=AX.X, op=ALU.add)
+            inv = soft.tile([P, NH, BLOCKS], F32)
+            nc.vector.reciprocal(out=inv[:], in_=total[:])
+            attn = soft.tile(spread, F32)
+            nc.vector.tensor_tensor(
+                out=attn[:], in0=expd[:], in1=inv[:].unsqueeze(2).to_broadcast(spread), op=ALU.mult
+            )
+            heads = soft.tile([P, NT, BLOCKS], F32)
+            nc.vector.tensor_reduce(
+                out=heads[:], in_=attn[:].rearrange("p n t k -> p t k n"), axis=AX.X, op=ALU.add
+            )
+            blocks = slice(BLOCKS * ch, BLOCKS * (ch + 1))
+            nc.vector.tensor_scalar(
+                out=result[:, blocks, :], in0=heads[:].rearrange("p t k -> p k t"), scalar1=1.0 / NH,
+                scalar2=None, op0=ALU.mult,
+            )
+            nc.sync.dma_start(
+                out=out_rows[CHUNK * ch : CHUNK * (ch + 1), :].rearrange("(k p) t -> p k t", p=P),
+                in_=result[:, blocks, :],
+            )
+
+        for b in range(B):
+            image_chunks = range(CHUNKS_IMAGE * b, CHUNKS_IMAGE * (b + 1))
+            for ch in image_chunks:
+                project("ref", ch)
+            for ch in image_chunks:
+                project("main", ch)
+                attention(ch)

@@ -26,7 +26,6 @@ BLOCKS = CHUNK // P
 ROWS_CHUNK = CHUNK // W
 HP = H + 2 * PAD
 WP = W + 2 * PAD
-PAIRS = NH // 2
 
 FLOPS = 2 * 2 * PIXELS * C * NH * D + 2 * NH * PIXELS * NT * D
 
@@ -49,7 +48,7 @@ def tile_reflocal7mh_e_kernel(
         soft = ctx.enter_context(tc.tile_pool(name="soft", bufs=2))
         ps_xt = ctx.enter_context(tc.psum_pool(name="ps_xt", bufs=2))
         ps_proj = ctx.enter_context(tc.psum_pool(name="ps_proj", bufs=2))
-        ps_score = ctx.enter_context(tc.psum_pool(name="ps_score", bufs=4))
+        ps_turn = ctx.enter_context(tc.psum_pool(name="ps_turn", bufs=4))
 
         def load_x(label, ch):
             x_sb = xpool.tile([P, BLOCKS, C], BF16)
@@ -89,8 +88,6 @@ def tile_reflocal7mh_e_kernel(
 
         ident = const.tile([P, P], F32)
         make_identity(nc, ident[:])
-        ones = const.tile([P, 2], F32)
-        nc.gpsimd.memset(ones[:], 1.0)
         x_codes = {}
         x_planes = {}
         for label in ("ref", "main"):
@@ -156,28 +153,30 @@ def tile_reflocal7mh_e_kernel(
             b, part = divmod(ch, CHUNKS_IMAGE)
             top = ROWS_CHUNK * part
             scores = soft.tile([P, NH, NT, BLOCKS], F32)
-            for pair in range(PAIRS):
-                s_ps = ps_score.tile([P, 2, NT, BLOCKS, 2], F32)
-                for i in range(2):
-                    n = 2 * pair + i
-                    for t in range(NT):
+            for n in range(NH):
+                q_chunk = q_sb[:, n, cols]
+                for t in range(NT):
+                    turned = ps_turn.tile([P, BLOCKS, P], F32)
+                    if t < NT - 1:
+                        di, dj = divmod(t, WIN)
                         prod = products.tile([P, CHUNK], F32)
-                        if t < NT - 1:
-                            di, dj = divmod(t, WIN)
-                            nc.vector.tensor_tensor(
-                                out=prod[:].rearrange("p (i j) -> p i j", j=W),
-                                in0=q_sb[:, n, cols].rearrange("p (i j) -> p i j", j=W),
-                                in1=k_image(n, b)[:, top + di : top + di + ROWS_CHUNK, dj : dj + W],
-                                op=ALU.mult,
-                            )
-                        else:
-                            nc.scalar.activation(out=prod[:], in_=q_sb[:, n, cols], func=ACT.Square)
-                        for k in range(BLOCKS):
-                            nc.tensor.matmul(
-                                out=s_ps[:, i, t, k, :], lhsT=prod[:, P * k : P * (k + 1)], rhs=ones[:],
-                                start=True, stop=True,
-                            )
-                nc.scalar.copy(out=scores[:, 2 * pair : 2 * pair + 2, :, :], in_=s_ps[:, :, :, :, 0])
+                        nc.vector.tensor_tensor(
+                            out=prod[:].rearrange("p (i j) -> p i j", j=W),
+                            in0=q_chunk.rearrange("p (i j) -> p i j", j=W),
+                            in1=k_image(n, b)[:, top + di : top + di + ROWS_CHUNK, dj : dj + W],
+                            op=ALU.mult,
+                        )
+                        source, func = prod[:], ACT.Copy
+                    else:
+                        source, func = q_chunk, ACT.Square
+                    for k in range(BLOCKS):
+                        nc.tensor.transpose(turned[:, k, :], source[:, P * k : P * (k + 1)], ident[:])
+                    for k in range(BLOCKS):
+                        unused = products.tile([P, P], F32)
+                        nc.scalar.activation(
+                            out=unused[:], in_=turned[:, k, :], func=func,
+                            accum_out=scores[:, n, t, k : k + 1],
+                        )
             by_t = "p n t k -> p n k t"
             spread = [P, NH, NT, BLOCKS]
             neg_max = soft.tile([P, NH, BLOCKS], F32)

@@ -26,6 +26,8 @@ BLOCKS = CHUNK // P
 ROWS_CHUNK = CHUNK // W
 HP = H + 2 * PAD
 WP = W + 2 * PAD
+VECTOR_SHARE = 6
+LINE = 8
 
 FLOPS = 2 * 2 * PIXELS * C * NH * D + 2 * NH * PIXELS * NT * D
 
@@ -152,7 +154,8 @@ def tile_reflocal7mh_e_kernel(
             cols = slice(CHUNK * ch, CHUNK * (ch + 1))
             b, part = divmod(ch, CHUNKS_IMAGE)
             top = ROWS_CHUNK * part
-            scores = soft.tile([P, NH, NT, BLOCKS], F32)
+            sums = soft.tile([P, NH, NT, LINE], F32)
+            scores = sums[:, :, :, 0:BLOCKS]
             for n in range(NH):
                 q_chunk = q_sb[:, n, cols]
                 for t in range(NT):
@@ -171,21 +174,26 @@ def tile_reflocal7mh_e_kernel(
                         source, func = q_chunk, ACT.Square
                     for k in range(BLOCKS):
                         nc.tensor.transpose(turned[:, k, :], source[:, P * k : P * (k + 1)], ident[:])
-                    for k in range(BLOCKS):
-                        unused = products.tile([P, P], F32)
-                        nc.scalar.activation(
-                            out=unused[:], in_=turned[:, k, :], func=func,
-                            accum_out=scores[:, n, t, k : k + 1],
+                    if t % VECTOR_SHARE == VECTOR_SHARE - 1:
+                        nc.vector.tensor_reduce(
+                            out=scores[:, n, t, :], in_=turned[:], axis=AX.X, op=ALU.add
                         )
+                    else:
+                        for k in range(BLOCKS):
+                            unused = products.tile([P, P], F32)
+                            nc.scalar.activation(
+                                out=unused[:], in_=turned[:, k, :], func=func,
+                                accum_out=scores[:, n, t, k : k + 1],
+                            )
             by_t = "p n t k -> p n k t"
             spread = [P, NH, NT, BLOCKS]
             neg_max = soft.tile([P, NH, BLOCKS], F32)
             nc.vector.tensor_reduce(
-                out=neg_max[:], in_=scores[:].rearrange(by_t), axis=AX.X, op=ALU.max, negate=True
+                out=neg_max[:], in_=scores.rearrange(by_t), axis=AX.X, op=ALU.max, negate=True
             )
             shifted = soft.tile(spread, F32)
             nc.vector.tensor_tensor(
-                out=shifted[:], in0=scores[:], in1=neg_max[:].unsqueeze(2).to_broadcast(spread),
+                out=shifted[:], in0=scores, in1=neg_max[:].unsqueeze(2).to_broadcast(spread),
                 op=ALU.add,
             )
             expd = soft.tile(spread, F32)

@@ -26,7 +26,6 @@ BLOCKS = CHUNK // P
 ROWS_CHUNK = CHUNK // W
 HP = H + 2 * PAD
 WP = W + 2 * PAD
-VECTOR_SHARE = 6
 LINE = 8
 
 FLOPS = 2 * 2 * PIXELS * C * NH * D + 2 * NH * PIXELS * NT * D
@@ -125,30 +124,31 @@ def tile_reflocal7mh_e_kernel(
                 in_=grouped[:],
             )
 
-        def project(label, ch):
-            quantise(label, ch)
+        def project(label, ch, n):
             cols = slice(CHUNK * ch, CHUNK * (ch + 1))
+            codes, plane = weights[label]
+            acc = ps_proj.tile([P, CHUNK], F32)
+            nc.tensor.matmul_mx(
+                out=acc[:],
+                lhsT=codes[:, n, :].bitcast(FP8X4),
+                lhsT_scale=plane[:, n, :],
+                rhs=x_codes[label][:, cols].bitcast(FP8X4),
+                rhs_scale=x_planes[label][:, cols],
+                start=True,
+                stop=True,
+            )
+            return acc
+
+        def keys(ch):
+            quantise("ref", ch)
             b, part = divmod(ch, CHUNKS_IMAGE)
             rows = slice(PAD + ROWS_CHUNK * part, PAD + ROWS_CHUNK * (part + 1))
-            codes, plane = weights[label]
             for n in range(NH):
-                acc = ps_proj.tile([P, CHUNK], F32)
-                nc.tensor.matmul_mx(
-                    out=acc[:],
-                    lhsT=codes[:, n, :].bitcast(FP8X4),
-                    lhsT_scale=plane[:, n, :],
-                    rhs=x_codes[label][:, cols].bitcast(FP8X4),
-                    rhs_scale=x_planes[label][:, cols],
-                    start=True,
-                    stop=True,
+                acc = project("ref", ch, n)
+                nc.scalar.copy(
+                    out=k_image(n, b)[:, rows, PAD : PAD + W],
+                    in_=acc[:].rearrange("p (i j) -> p i j", j=W),
                 )
-                if label == "ref":
-                    nc.scalar.copy(
-                        out=k_image(n, b)[:, rows, PAD : PAD + W],
-                        in_=acc[:].rearrange("p (i j) -> p i j", j=W),
-                    )
-                else:
-                    nc.scalar.copy(out=q_sb[:, n, cols], in_=acc[:])
 
         def attention(ch):
             cols = slice(CHUNK * ch, CHUNK * (ch + 1))
@@ -156,25 +156,37 @@ def tile_reflocal7mh_e_kernel(
             top = ROWS_CHUNK * part
             sums = soft.tile([P, NH, NT, LINE], F32)
             scores = sums[:, :, :, 0:BLOCKS]
+            quantise("main", ch)
             for n in range(NH):
+                q_psum = project("main", ch, n)
                 q_chunk = q_sb[:, n, cols]
+                nc.scalar.copy(out=q_chunk, in_=q_psum[:])
                 for t in range(NT):
                     turned = ps_turn.tile([P, BLOCKS, P], F32)
                     if t < NT - 1:
                         di, dj = divmod(t, WIN)
                         prod = products.tile([P, CHUNK], F32)
-                        nc.vector.tensor_tensor(
-                            out=prod[:].rearrange("p (i j) -> p i j", j=W),
-                            in0=q_chunk.rearrange("p (i j) -> p i j", j=W),
-                            in1=k_image(n, b)[:, top + di : top + di + ROWS_CHUNK, dj : dj + W],
-                            op=ALU.mult,
-                        )
+                        window = k_image(n, b)[:, top + di : top + di + ROWS_CHUNK, dj : dj + W]
+                        if t % 3 == 2:
+                            nc.gpsimd.tensor_tensor(
+                                out=prod[:].rearrange("p (i j) -> p i j", j=W),
+                                in0=q_chunk.rearrange("p (i j) -> p i j", j=W),
+                                in1=window,
+                                op=ALU.mult,
+                            )
+                        else:
+                            nc.vector.tensor_tensor(
+                                out=prod[:].rearrange("p (i j) -> p i j", j=W),
+                                in0=q_psum[:].rearrange("p (i j) -> p i j", j=W),
+                                in1=window,
+                                op=ALU.mult,
+                            )
                         source, func = prod[:], ACT.Copy
                     else:
                         source, func = q_chunk, ACT.Square
                     for k in range(BLOCKS):
                         nc.tensor.transpose(turned[:, k, :], source[:, P * k : P * (k + 1)], ident[:])
-                    if t % VECTOR_SHARE == VECTOR_SHARE - 1:
+                    if t % 3 == 0:
                         nc.vector.tensor_reduce(
                             out=scores[:, n, t, :], in_=turned[:], axis=AX.X, op=ALU.add
                         )
@@ -223,7 +235,6 @@ def tile_reflocal7mh_e_kernel(
         for b in range(B):
             image_chunks = range(CHUNKS_IMAGE * b, CHUNKS_IMAGE * (b + 1))
             for ch in image_chunks:
-                project("ref", ch)
+                keys(ch)
             for ch in image_chunks:
-                project("main", ch)
                 attention(ch)

@@ -26,6 +26,7 @@ BLOCKS = CHUNK // P
 ROWS_CHUNK = CHUNK // W
 HP = H + 2 * PAD
 WP = W + 2 * PAD
+VECTOR_SHARE = 5
 LINE = 8
 
 FLOPS = 2 * 2 * PIXELS * C * NH * D + 2 * NH * PIXELS * NT * D
@@ -102,6 +103,12 @@ def tile_reflocal7mh_e_kernel(
         def k_image(n, b):
             return k_sb[:, n * B + b, :].rearrange("p (i j) -> p i j", j=WP)
 
+        def copy_out(label, ch, piece, out_ap, in_ap):
+            if label == "ref" and ch < CHUNKS_IMAGE and piece % 2 == 0:
+                nc.vector.tensor_copy(out=out_ap, in_=in_ap)
+            else:
+                nc.scalar.copy(out=out_ap, in_=in_ap)
+
         def quantise(label, ch):
             words = x_tiles[(label, ch)][:].bitcast(F32)
             grouped = stage.tile([P, 4 * CHUNK], BF16, align_bytes=64)
@@ -113,9 +120,12 @@ def tile_reflocal7mh_e_kernel(
                         nc.tensor.transpose(
                             xt[:, k, u, :], words[:, 2 * half + k, u : C // 2 : 2], ident[:]
                         )
-                nc.scalar.copy(
-                    out=grouped_words[:, 2 * half : 2 * half + 2, :, :],
-                    in_=xt[:].rearrange("p k u r -> p k r u"),
+                copy_out(
+                    label,
+                    ch,
+                    half,
+                    grouped_words[:, 2 * half : 2 * half + 2, :, :],
+                    xt[:].rearrange("p k u r -> p k r u"),
                 )
             cols = slice(CHUNK * ch, CHUNK * (ch + 1))
             nc.vector.quantize_mx(
@@ -124,31 +134,33 @@ def tile_reflocal7mh_e_kernel(
                 in_=grouped[:],
             )
 
-        def project(label, ch, n):
+        def project(label, ch):
+            quantise(label, ch)
             cols = slice(CHUNK * ch, CHUNK * (ch + 1))
-            codes, plane = weights[label]
-            acc = ps_proj.tile([P, CHUNK], F32)
-            nc.tensor.matmul_mx(
-                out=acc[:],
-                lhsT=codes[:, n, :].bitcast(FP8X4),
-                lhsT_scale=plane[:, n, :],
-                rhs=x_codes[label][:, cols].bitcast(FP8X4),
-                rhs_scale=x_planes[label][:, cols],
-                start=True,
-                stop=True,
-            )
-            return acc
-
-        def keys(ch):
-            quantise("ref", ch)
             b, part = divmod(ch, CHUNKS_IMAGE)
             rows = slice(PAD + ROWS_CHUNK * part, PAD + ROWS_CHUNK * (part + 1))
+            codes, plane = weights[label]
             for n in range(NH):
-                acc = project("ref", ch, n)
-                nc.scalar.copy(
-                    out=k_image(n, b)[:, rows, PAD : PAD + W],
-                    in_=acc[:].rearrange("p (i j) -> p i j", j=W),
+                acc = ps_proj.tile([P, CHUNK], F32)
+                nc.tensor.matmul_mx(
+                    out=acc[:],
+                    lhsT=codes[:, n, :].bitcast(FP8X4),
+                    lhsT_scale=plane[:, n, :],
+                    rhs=x_codes[label][:, cols].bitcast(FP8X4),
+                    rhs_scale=x_planes[label][:, cols],
+                    start=True,
+                    stop=True,
                 )
+                if label == "ref":
+                    copy_out(
+                        label,
+                        ch,
+                        n,
+                        k_image(n, b)[:, rows, PAD : PAD + W],
+                        acc[:].rearrange("p (i j) -> p i j", j=W),
+                    )
+                else:
+                    nc.scalar.copy(out=q_sb[:, n, cols], in_=acc[:])
 
         def attention(ch):
             cols = slice(CHUNK * ch, CHUNK * (ch + 1))
@@ -156,37 +168,25 @@ def tile_reflocal7mh_e_kernel(
             top = ROWS_CHUNK * part
             sums = soft.tile([P, NH, NT, LINE], F32)
             scores = sums[:, :, :, 0:BLOCKS]
-            quantise("main", ch)
             for n in range(NH):
-                q_psum = project("main", ch, n)
                 q_chunk = q_sb[:, n, cols]
-                nc.scalar.copy(out=q_chunk, in_=q_psum[:])
                 for t in range(NT):
                     turned = ps_turn.tile([P, BLOCKS, P], F32)
                     if t < NT - 1:
                         di, dj = divmod(t, WIN)
                         prod = products.tile([P, CHUNK], F32)
-                        window = k_image(n, b)[:, top + di : top + di + ROWS_CHUNK, dj : dj + W]
-                        if t % 3 == 2:
-                            nc.gpsimd.tensor_tensor(
-                                out=prod[:].rearrange("p (i j) -> p i j", j=W),
-                                in0=q_chunk.rearrange("p (i j) -> p i j", j=W),
-                                in1=window,
-                                op=ALU.mult,
-                            )
-                        else:
-                            nc.vector.tensor_tensor(
-                                out=prod[:].rearrange("p (i j) -> p i j", j=W),
-                                in0=q_psum[:].rearrange("p (i j) -> p i j", j=W),
-                                in1=window,
-                                op=ALU.mult,
-                            )
+                        nc.vector.tensor_tensor(
+                            out=prod[:].rearrange("p (i j) -> p i j", j=W),
+                            in0=q_chunk.rearrange("p (i j) -> p i j", j=W),
+                            in1=k_image(n, b)[:, top + di : top + di + ROWS_CHUNK, dj : dj + W],
+                            op=ALU.mult,
+                        )
                         source, func = prod[:], ACT.Copy
                     else:
                         source, func = q_chunk, ACT.Square
                     for k in range(BLOCKS):
                         nc.tensor.transpose(turned[:, k, :], source[:, P * k : P * (k + 1)], ident[:])
-                    if t % 3 == 0:
+                    if t % VECTOR_SHARE == VECTOR_SHARE - 1:
                         nc.vector.tensor_reduce(
                             out=scores[:, n, t, :], in_=turned[:], axis=AX.X, op=ALU.add
                         )
@@ -235,6 +235,7 @@ def tile_reflocal7mh_e_kernel(
         for b in range(B):
             image_chunks = range(CHUNKS_IMAGE * b, CHUNKS_IMAGE * (b + 1))
             for ch in image_chunks:
-                keys(ch)
+                project("ref", ch)
             for ch in image_chunks:
+                project("main", ch)
                 attention(ch)

from contextlib import ExitStack

import concourse.mybir as mybir
from concourse.masks import make_identity

F32 = mybir.dt.float32
BF16 = mybir.dt.bfloat16
I32 = mybir.dt.int32
U32 = mybir.dt.uint32
U8 = mybir.dt.uint8
FP8X4 = mybir.dt.float8_e4m3fn_x4
ALU = mybir.AluOpType
ACT = mybir.ActivationFunctionType
AX = mybir.AxisListType

P = 128
B, H, W, C, NH, D = 2, 32, 32, 512, 4, 128
WIN = 5
PAD = WIN // 2
NT = WIN * WIN + 1
PIXELS = B * H * W
CHUNK = 512
N_CHUNKS = PIXELS // CHUNK
CHUNKS_IMAGE = N_CHUNKS // B
BLOCKS = CHUNK // P
ROWS_CHUNK = CHUNK // W
HP = H + 2 * PAD
WP = W + 2 * PAD
VECTOR_SHARE = 5
LINE = 8

FLOPS = 2 * 2 * PIXELS * C * NH * D + 2 * NH * PIXELS * NT * D


def tile_reflocal7mh_e_kernel(
    tc, main, ref, W_main_words, W_main_scales, W_ref_words, W_ref_scales, out
):
    nc = tc.nc
    x_rows = {
        "ref": ref.rearrange("b i j c -> (b i j) c"),
        "main": main.rearrange("b i j c -> (b i j) c"),
    }
    out_rows = out.rearrange("b i j t -> (b i j) t")

    with ExitStack() as ctx:
        const = ctx.enter_context(tc.tile_pool(name="const", bufs=1))
        xpool = ctx.enter_context(tc.tile_pool(name="xpool", bufs=2 * N_CHUNKS))
        stage = ctx.enter_context(tc.tile_pool(name="stage", bufs=2))
        products = ctx.enter_context(tc.tile_pool(name="products", bufs=4))
        soft = ctx.enter_context(tc.tile_pool(name="soft", bufs=2))
        ps_xt = ctx.enter_context(tc.psum_pool(name="ps_xt", bufs=2))
        ps_proj = ctx.enter_context(tc.psum_pool(name="ps_proj", bufs=2))
        ps_turn = ctx.enter_context(tc.psum_pool(name="ps_turn", bufs=4))

        def load_x(label, ch):
            x_sb = xpool.tile([P, BLOCKS, C], BF16)
            nc.sync.dma_start(
                out=x_sb[:],
                in_=x_rows[label][CHUNK * ch : CHUNK * (ch + 1), :].rearrange(
                    "(k p) c -> p k c", p=P
                ),
            )
            return x_sb

        def load_weight(words, scales, label):
            codes = const.tile([P, NH, D], U32, align_bytes=64, name="codes_" + label)
            nc.sync.dma_start(
                out=codes[:].bitcast(I32),
                in_=words.rearrange("g p n t -> g p (n t)").bitcast(I32).rearrange("g p n -> p g n"),
            )
            plane = const.tile([P, NH, D], U8, align_bytes=64, name="plane_" + label)
            nc.vector.memset(plane[:].bitcast(I32), 0)
            scale_words = scales.bitcast(I32)
            for quad in range(4):
                nc.sync.dma_start(
                    out=plane[:].bitcast(I32)[32 * quad : 32 * quad + 4, :, :],
                    in_=scale_words[:, 4 * quad : 4 * quad + 4, :].rearrange("g r n -> r g n"),
                )
            return codes, plane

        w_inputs = {"ref": (W_ref_words, W_ref_scales), "main": (W_main_words, W_main_scales)}
        x_tiles = {}
        weights = {}
        for b in range(B):
            for label in ("ref", "main"):
                for ch in range(CHUNKS_IMAGE * b, CHUNKS_IMAGE * (b + 1)):
                    x_tiles[(label, ch)] = load_x(label, ch)
                    if ch == 0:
                        weights[label] = load_weight(w_inputs[label][0], w_inputs[label][1], label)

        ident = const.tile([P, P], F32)
        make_identity(nc, ident[:])
        x_codes = {}
        x_planes = {}
        for label in ("ref", "main"):
            x_codes[label] = const.tile([P, PIXELS], U32, align_bytes=64, name="xcodes_" + label)
            x_planes[label] = const.tile([P, PIXELS], U8, align_bytes=64, name="xplane_" + label)
        q_sb = const.tile([P, NH, PIXELS], F32)
        k_sb = const.tile([P, NH * B, HP * WP], F32)
        nc.vector.memset(k_sb[:], 0.0)
        result = const.tile([P, N_CHUNKS * BLOCKS, NT], F32)

        def k_image(n, b):
            return k_sb[:, n * B + b, :].rearrange("p (i j) -> p i j", j=WP)

        def copy_out(label, ch, piece, out_ap, in_ap):
            if label == "ref" and ch < CHUNKS_IMAGE and piece % 2 == 0:
                nc.vector.tensor_copy(out=out_ap, in_=in_ap)
            else:
                nc.scalar.copy(out=out_ap, in_=in_ap)

        def quantise(label, ch):
            words = x_tiles[(label, ch)][:].bitcast(F32)
            grouped = stage.tile([P, 4 * CHUNK], BF16, align_bytes=64)
            grouped_words = grouped[:].bitcast(F32).rearrange("p (k r u) -> p k r u", r=P, u=2)
            for half in range(BLOCKS // 2):
                xt = ps_xt.tile([P, 2, 2, P], F32)
                for k in range(2):
                    for u in range(2):
                        nc.tensor.transpose(
                            xt[:, k, u, :], words[:, 2 * half + k, u : C // 2 : 2], ident[:]
                        )
                copy_out(
                    label,
                    ch,
                    half,
                    grouped_words[:, 2 * half : 2 * half + 2, :, :],
                    xt[:].rearrange("p k u r -> p k r u"),
                )
            cols = slice(CHUNK * ch, CHUNK * (ch + 1))
            nc.vector.quantize_mx(
                out=x_codes[label][:, cols].bitcast(FP8X4),
                scales=x_planes[label][:, cols],
                in_=grouped[:],
            )

        def project(label, ch):
            quantise(label, ch)
            cols = slice(CHUNK * ch, CHUNK * (ch + 1))
            b, part = divmod(ch, CHUNKS_IMAGE)
            rows = slice(PAD + ROWS_CHUNK * part, PAD + ROWS_CHUNK * (part + 1))
            codes, plane = weights[label]
            for n in range(NH):
                acc = ps_proj.tile([P, CHUNK], F32)
                nc.tensor.matmul_mx(
                    out=acc[:],
                    lhsT=codes[:, n, :].bitcast(FP8X4),
                    lhsT_scale=plane[:, n, :],
                    rhs=x_codes[label][:, cols].bitcast(FP8X4),
                    rhs_scale=x_planes[label][:, cols],
                    start=True,
                    stop=True,
                )
                if label == "ref":
                    copy_out(
                        label,
                        ch,
                        n,
                        k_image(n, b)[:, rows, PAD : PAD + W],
                        acc[:].rearrange("p (i j) -> p i j", j=W),
                    )
                else:
                    nc.scalar.copy(out=q_sb[:, n, cols], in_=acc[:])

        def attention(ch):
            cols = slice(CHUNK * ch, CHUNK * (ch + 1))
            b, part = divmod(ch, CHUNKS_IMAGE)
            top = ROWS_CHUNK * part
            sums = soft.tile([P, NH, NT, LINE], F32)
            scores = sums[:, :, :, 0:BLOCKS]
            for n in range(NH):
                q_chunk = q_sb[:, n, cols]
                for t in range(NT):
                    turned = ps_turn.tile([P, BLOCKS, P], F32)
                    if t < NT - 1:
                        di, dj = divmod(t, WIN)
                        prod = products.tile([P, CHUNK], F32)
                        nc.vector.tensor_tensor(
                            out=prod[:].rearrange("p (i j) -> p i j", j=W),
                            in0=q_chunk.rearrange("p (i j) -> p i j", j=W),
                            in1=k_image(n, b)[:, top + di : top + di + ROWS_CHUNK, dj : dj + W],
                            op=ALU.mult,
                        )
                        source, func = prod[:], ACT.Copy
                    else:
                        source, func = q_chunk, ACT.Square
                    for k in range(BLOCKS):
                        nc.tensor.transpose(turned[:, k, :], source[:, P * k : P * (k + 1)], ident[:])
                    if t % VECTOR_SHARE == VECTOR_SHARE - 1:
                        nc.vector.tensor_reduce(
                            out=scores[:, n, t, :], in_=turned[:], axis=AX.X, op=ALU.add
                        )
                    else:
                        for k in range(BLOCKS):
                            unused = products.tile([P, P], F32)
                            nc.scalar.activation(
                                out=unused[:], in_=turned[:, k, :], func=func,
                                accum_out=scores[:, n, t, k : k + 1],
                            )
            by_t = "p n t k -> p n k t"
            spread = [P, NH, NT, BLOCKS]
            neg_max = soft.tile([P, NH, BLOCKS], F32)
            nc.vector.tensor_reduce(
                out=neg_max[:], in_=scores.rearrange(by_t), axis=AX.X, op=ALU.max, negate=True
            )
            shifted = soft.tile(spread, F32)
            nc.vector.tensor_tensor(
                out=shifted[:], in0=scores, in1=neg_max[:].unsqueeze(2).to_broadcast(spread),
                op=ALU.add,
            )
            expd = soft.tile(spread, F32)
            nc.scalar.activation(out=expd[:], in_=shifted[:], func=ACT.Exp)
            total = soft.tile([P, NH, BLOCKS], F32)
            nc.vector.tensor_reduce(out=total[:], in_=expd[:].rearrange(by_t), axis=AX.X, op=ALU.add)
            inv = soft.tile([P, NH, BLOCKS], F32)
            nc.vector.reciprocal(out=inv[:], in_=total[:])
            attn = soft.tile(spread, F32)
            nc.vector.tensor_tensor(
                out=attn[:], in0=expd[:], in1=inv[:].unsqueeze(2).to_broadcast(spread), op=ALU.mult
            )
            heads = soft.tile([P, NT, BLOCKS], F32)
            nc.vector.tensor_reduce(
                out=heads[:], in_=attn[:].rearrange("p n t k -> p t k n"), axis=AX.X, op=ALU.add
            )
            blocks = slice(BLOCKS * ch, BLOCKS * (ch + 1))
            nc.vector.tensor_scalar(
                out=result[:, blocks, :], in0=heads[:].rearrange("p t k -> p k t"), scalar1=1.0 / NH,
                scalar2=None, op0=ALU.mult,
            )
            nc.sync.dma_start(
                out=out_rows[CHUNK * ch : CHUNK * (ch + 1), :].rearrange("(k p) t -> p k t", p=P),
                in_=result[:, blocks, :],
            )

        for b in range(B):
            image_chunks = range(CHUNKS_IMAGE * b, CHUNKS_IMAGE * (b + 1))
            for ch in image_chunks:
                project("ref", ch)
            for ch in image_chunks:
                project("main", ch)
                attention(ch)
